import numpy as np
import ml_dtypes


def mxq(x, axis, fmt="e4m3"):
    dtype, down = {"e4m3": (ml_dtypes.float8_e4m3fn, 7), "e5m2": (ml_dtypes.float8_e5m2, 14)}[fmt]
    v = np.moveaxis(np.asarray(x, np.float32).astype(ml_dtypes.bfloat16).astype(np.float64), axis, -1)
    blocks = v.reshape(v.shape[:-1] + (-1, 32))
    amax = np.abs(blocks).max(-1, keepdims=True)
    byte = np.maximum(np.where(amax > 0, np.frexp(amax)[1] - 1 + 127, 0) - down, 1)
    scale = np.exp2(byte - 127.0)
    codes = (blocks / scale).astype(np.float32).astype(dtype).astype(np.float64)
    return np.moveaxis((codes * scale).reshape(v.shape), -1, axis)


WIDE = False


def mx_kscale(k):
    if not WIDE:
        return np.ones(k)
    levels = np.array([10, -10, 5, -5, 0])
    a = np.random.permutation(np.resize(levels, k // 512 * 4)).reshape(k // 512, 4)
    idx = np.arange(k)
    return np.exp2(a[idx // 512, idx % 128 // 32])


BF16 = ml_dtypes.bfloat16


def bf(x):
    return np.asarray(x, np.float32).astype(BF16)


def f64(x):
    return np.asarray(x).astype(np.float64)


E2M1 = np.array([0.0, 0.5, 1.0, 1.5, 2.0, 3.0, 4.0, 6.0, -0.0, -0.5, -1.0, -1.5, -2.0, -3.0, -4.0, -6.0])


def pack_weight(w, fmt):
    k, n = w.shape
    w = f64(bf(w)).reshape(k // 32, 32, n)
    amax = np.abs(w).max(1)
    if fmt == "e4m3":
        byte = np.frexp(amax)[1] - 1 + 127 - 7
    else:
        mant, ex = np.frexp(amax / 6.0)
        byte = np.where(mant > 0.5, ex, ex - 1) + 127
    byte = np.clip(np.where(amax > 0, byte, 1), 1, 254)
    scaled = (w * np.exp2(127.0 - byte)[:, None, :]).reshape(k, n).astype(np.float32)
    by_word = np.ascontiguousarray(scaled.reshape(k // 512, 128, 4, n).transpose(0, 1, 3, 2))
    if fmt == "e4m3":
        words = by_word.astype(ml_dtypes.float8_e4m3fn).view(np.uint8)
    else:
        c = by_word.astype(ml_dtypes.float4_e2m1fn).view(np.uint8) & 0xF
        words = c[..., 0::2] | (c[..., 1::2] << 4)
    return np.ascontiguousarray(words), np.ascontiguousarray(byte.astype(np.uint8).reshape(k // 512, 16, n))


def unpack_weight(words, scales, fmt):
    g, p, n, _ = words.shape
    if fmt == "e4m3":
        vals = np.ascontiguousarray(words).view(ml_dtypes.float8_e4m3fn).astype(np.float64)
    else:
        nib = np.empty((g, p, n, 4), np.uint8)
        nib[..., 0::2] = words & 0xF
        nib[..., 1::2] = words >> 4
        vals = E2M1[nib]
    vals = vals * np.repeat(np.exp2(scales.astype(np.float64) - 127.0), 8, axis=1)[..., None]
    return vals.transpose(0, 1, 3, 2).reshape(g * 512, n)


N, LMAX, CIN, COUT = 512, 3, 1024, 128
NL = LMAX + 1
NM = NL * NL


def setup_inputs():
    s = mx_kscale(CIN)
    x = bf(np.random.standard_normal((N, NM, CIN)) * s)
    stack = np.random.standard_normal((NL, CIN, COUT)) / np.sqrt(CIN) / s[:, None]
    words, scales = pack_weight(stack.reshape(-1, COUT), "e4m3")
    path_weights = bf(1.0 + 0.3 * np.random.standard_normal(NL))
    return {"x": x,
            "weights_words": words,
            "weights_scales": scales,
            "path_weights": path_weights}


def reference(x, weights_words, weights_scales, path_weights):
    x, path_weights = f64(x), f64(path_weights)
    weights = unpack_weight(weights_words, weights_scales, "e4m3").reshape(NL, CIN, COUT)
    blocks = []
    for l in range(LMAX + 1):
        start = l * l
        end = start + (2 * l + 1)
        blk = mxq(x[:, start:end, :], 2, "e4m3") @ weights[l]
        blocks.append(path_weights[l] * blk)
    return np.concatenate(blocks, axis=1)

@@ -1,0 +1,156 @@
+from contextlib import ExitStack
+
+import concourse.mybir as mybir
+from concourse.masks import make_identity
+
+BF16 = mybir.dt.bfloat16
+F32 = mybir.dt.float32
+I32 = mybir.dt.int32
+U32 = mybir.dt.uint32
+U8 = mybir.dt.uint8
+FP8X4 = mybir.dt.float8_e4m3fn_x4
+
+NODES, ROWS, CIN, COUT, DEGREES = 512, 16, 1024, 128, 4
+DEGREE_OF_ROW = [l for l in range(DEGREES) for i in range(2 * l + 1)]
+assert len(DEGREE_OF_ROW) == ROWS
+
+P = 128
+PACK = 4
+K_PASS = P * PACK
+PASSES = CIN // K_PASS
+HALVES = 2
+QUADRANTS = 4
+
+PAIR = 2
+ROUND = 4
+PAIRS_PER_ROUND = ROUND // PAIR
+ROUNDS_PER_NODE_TILE = ROWS // ROUND
+N_ROUNDS = (NODES // P) * ROUNDS_PER_NODE_TILE
+N_PAIRS = N_ROUNDS * PAIRS_PER_ROUND
+PAIRS_BEFORE_WEIGHTS = 2 * PAIRS_PER_ROUND
+
+FLOPS = 2 * NODES * ROWS * CIN * COUT
+
+
+def tile_linear_pa_t_e_kernel(tc, x, weights_words, weights_scales, path_weights, out):
+    nc = tc.nc
+    with ExitStack() as ctx:
+        ctx.enter_context(tc.manual_schedule())
+        consts = ctx.enter_context(tc.tile_pool(name="consts", bufs=1))
+        x_pool = ctx.enter_context(tc.tile_pool(name="x", bufs=N_PAIRS))
+        grouped_pool = ctx.enter_context(tc.tile_pool(name="grouped", bufs=2 * PAIRS_PER_ROUND))
+        codes_pool = ctx.enter_context(tc.tile_pool(name="codes", bufs=3 * PAIRS_PER_ROUND))
+        result_pool = ctx.enter_context(tc.tile_pool(name="result", bufs=N_ROUNDS))
+        turned_pool = ctx.enter_context(tc.psum_pool(name="turned", bufs=6))
+        acc_pool = ctx.enter_context(tc.psum_pool(name="acc", bufs=2))
+
+        def node_rows(r):
+            first = (r // ROUNDS_PER_NODE_TILE) * P
+            return slice(first, first + P)
+
+        def first_row(r):
+            return (r % ROUNDS_PER_NODE_TILE) * ROUND
+
+        identity = consts.tile([P, P], F32)
+        make_identity(nc, identity[:])
+
+        factor_of_degree = consts.tile([P, DEGREES], BF16)
+        nc.scalar.dma_start(out=factor_of_degree[:], in_=path_weights.partition_broadcast(P))
+        factor_of_row = consts.tile([P, ROWS], F32)
+
+        w_codes = consts.tile([P, DEGREES * PASSES, COUT], U32, align_bytes=64)
+        w_scales = consts.tile([P, DEGREES * PASSES, COUT], U8, align_bytes=64)
+        nc.vector.memset(w_scales[:].bitcast(I32), 0)
+
+        def load_weights():
+            nc.sync.dma_start(
+                out=w_codes[:].bitcast(I32),
+                in_=weights_words.rearrange("g p n t -> p g (n t)").bitcast(I32),
+            )
+            for quadrant in range(QUADRANTS):
+                nc.sync.dma_start(
+                    out=w_scales[32 * quadrant : 32 * quadrant + 4, :, :].bitcast(I32),
+                    in_=weights_scales[:, 4 * quadrant : 4 * quadrant + 4, :]
+                    .rearrange("g r n -> r g n")
+                    .bitcast(I32),
+                )
+
+        x_pairs = []
+        for pair in range(N_PAIRS):
+            if pair == PAIRS_BEFORE_WEIGHTS:
+                load_weights()
+            r = pair // PAIRS_PER_ROUND
+            row = first_row(r) + (pair % PAIRS_PER_ROUND) * PAIR
+            x_sb = x_pool.tile([P, PAIR, CIN], BF16)
+            nc.sync.dma_start(out=x_sb[:], in_=x[node_rows(r), row : row + PAIR, :])
+            x_pairs.append(x_sb)
+
+        for l in range(DEGREES):
+            rows_of_l = slice(l * l, (l + 1) * (l + 1))
+            nc.vector.tensor_copy(
+                out=factor_of_row[:, rows_of_l],
+                in_=factor_of_degree[:, l : l + 1].to_broadcast([P, 2 * l + 1]),
+            )
+
+        def transpose_and_quantise(r):
+            quantised = []
+            for pair in range(r * PAIRS_PER_ROUND, (r + 1) * PAIRS_PER_ROUND):
+                x_words = x_pairs[pair][:].bitcast(F32)
+                grouped = grouped_pool.tile([P, PAIR, PASSES, P, PACK], BF16, align_bytes=64)
+                for s in range(PAIR):
+                    turned = turned_pool.tile([P, PASSES, HALVES, P], F32)
+                    for g in range(PASSES):
+                        for u in range(HALVES):
+                            first_word = g * K_PASS // 2 + u
+                            nc.tensor.transpose(
+                                turned[:, g, u, :],
+                                x_words[:, s, first_word : (g + 1) * K_PASS // 2 : HALVES],
+                                identity[:],
+                            )
+                    nc.scalar.copy(
+                        out=grouped[:, s].bitcast(F32),
+                        in_=turned[:].rearrange("p g u n -> p g n u"),
+                    )
+                codes = codes_pool.tile([P, PAIR, PASSES, P], U32, align_bytes=64)
+                scales = codes_pool.tile([P, PAIR, PASSES, P], U8, align_bytes=64)
+                nc.vector.quantize_mx(
+                    out=codes[:].rearrange("p s g n -> p (s g n)").bitcast(FP8X4),
+                    scales=scales[:].rearrange("p s g n -> p (s g n)"),
+                    in_=grouped[:].rearrange("p s g n t -> p (s g n t)"),
+                )
+                quantised.append((codes, scales))
+            return quantised
+
+        def multiply_and_store(r, quantised):
+            acc = acc_pool.tile([P, ROUND, COUT], F32)
+            for slab in range(ROUND):
+                codes, scales = quantised[slab // PAIR]
+                s = slab % PAIR
+                l = DEGREE_OF_ROW[first_row(r) + slab]
+                for g in range(PASSES):
+                    nc.tensor.matmul_mx(
+                        out=acc[:, slab, :],
+                        lhsT=codes[:, s, g, :].bitcast(FP8X4),
+                        lhsT_scale=scales[:, s, g, :],
+                        rhs=w_codes[:, l * PASSES + g, :].bitcast(FP8X4),
+                        rhs_scale=w_scales[:, l * PASSES + g, :],
+                        start=(g == 0),
+                        stop=(g == PASSES - 1),
+                    )
+            rows = slice(first_row(r), first_row(r) + ROUND)
+            result = result_pool.tile([P, ROUND, COUT], F32)
+            nc.vector.tensor_tensor(
+                out=result[:],
+                in0=acc[:],
+                in1=factor_of_row[:, rows].unsqueeze(2).to_broadcast([P, ROUND, COUT]),
+                op=mybir.AluOpType.mult,
+            )
+            nc.sync.dma_start(out=out[node_rows(r), rows, :], in_=result[:])
+
+        waiting = None
+        for r in range(N_ROUNDS):
+            quantised = transpose_and_quantise(r)
+            if waiting is not None:
+                multiply_and_store(r - 1, waiting)
+            waiting = quantised
+        multiply_and_store(N_ROUNDS - 1, waiting)

@@ -18,6 +18,7 @@ P = 128
 PACK = 4
 K_PASS = P * PACK
 PASSES = CIN // K_PASS
+assert PASSES == 2
 HALVES = 2
 QUADRANTS = 4
 
@@ -38,6 +39,7 @@ def tile_linear_pa_t_e_kernel(tc, x, weights_words, weights_scales, path_weights
         ctx.enter_context(tc.manual_schedule())
         consts = ctx.enter_context(tc.tile_pool(name="consts", bufs=1))
         x_pool = ctx.enter_context(tc.tile_pool(name="x", bufs=N_PAIRS))
+        sorted_pool = ctx.enter_context(tc.tile_pool(name="sorted", bufs=3 * PAIRS_PER_ROUND))
         grouped_pool = ctx.enter_context(tc.tile_pool(name="grouped", bufs=2 * PAIRS_PER_ROUND))
         codes_pool = ctx.enter_context(tc.tile_pool(name="codes", bufs=3 * PAIRS_PER_ROUND))
         result_pool = ctx.enter_context(tc.tile_pool(name="result", bufs=N_ROUNDS))
@@ -92,21 +94,36 @@ def tile_linear_pa_t_e_kernel(tc, x, weights_words, weights_scales, path_weights
                 in_=factor_of_degree[:, l : l + 1].to_broadcast([P, 2 * l + 1]),
             )
 
-        def transpose_and_quantise(r):
+        def pairs_of(r):
+            return range(r * PAIRS_PER_ROUND, (r + 1) * PAIRS_PER_ROUND)
+
+        def sort_pass_0(r):
+            sorted_pairs = []
+            for pair in pairs_of(r):
+                x_words = x_pairs[pair][:].bitcast(F32)
+                sorted_words = sorted_pool.tile([P, PAIR, HALVES, P], F32)
+                nc.vector.tensor_copy(
+                    out=sorted_words[:],
+                    in_=x_words[:, :, 0 : K_PASS // 2].rearrange("p s (j u) -> p s u j", u=HALVES),
+                )
+                sorted_pairs.append(sorted_words)
+            return sorted_pairs
+
+        def transpose_and_quantise(r, sorted_pairs):
             quantised = []
-            for pair in range(r * PAIRS_PER_ROUND, (r + 1) * PAIRS_PER_ROUND):
+            for pair, sorted_words in zip(pairs_of(r), sorted_pairs):
                 x_words = x_pairs[pair][:].bitcast(F32)
                 grouped = grouped_pool.tile([P, PAIR, PASSES, P, PACK], BF16, align_bytes=64)
                 for s in range(PAIR):
                     turned = turned_pool.tile([P, PASSES, HALVES, P], F32)
-                    for g in range(PASSES):
-                        for u in range(HALVES):
-                            first_word = g * K_PASS // 2 + u
-                            nc.tensor.transpose(
-                                turned[:, g, u, :],
-                                x_words[:, s, first_word : (g + 1) * K_PASS // 2 : HALVES],
-                                identity[:],
-                            )
+                    for u in range(HALVES):
+                        nc.tensor.transpose(turned[:, 0, u, :], sorted_words[:, s, u, :], identity[:])
+                    for u in range(HALVES):
+                        nc.tensor.transpose(
+                            turned[:, 1, u, :],
+                            x_words[:, s, K_PASS // 2 + u : K_PASS : HALVES],
+                            identity[:],
+                        )
                     nc.scalar.copy(
                         out=grouped[:, s].bitcast(F32),
                         in_=turned[:].rearrange("p g u n -> p g n u"),
@@ -147,9 +164,13 @@ def tile_linear_pa_t_e_kernel(tc, x, weights_words, weights_scales, path_weights
             )
             nc.sync.dma_start(out=out[node_rows(r), rows, :], in_=result[:])
 
+        sorted_ahead = sort_pass_0(0)
         waiting = None
         for r in range(N_ROUNDS):
-            quantised = transpose_and_quantise(r)
+            sorted_now = sorted_ahead
+            if r + 1 < N_ROUNDS:
+                sorted_ahead = sort_pass_0(r + 1)
+            quantised = transpose_and_quantise(r, sorted_now)
             if waiting is not None:
                 multiply_and_store(r - 1, waiting)
             waiting = quantised

@@ -28,7 +28,7 @@ PAIRS_PER_ROUND = ROUND // PAIR
 ROUNDS_PER_NODE_TILE = ROWS // ROUND
 N_ROUNDS = (NODES // P) * ROUNDS_PER_NODE_TILE
 N_PAIRS = N_ROUNDS * PAIRS_PER_ROUND
-PAIRS_BEFORE_WEIGHTS = 2 * PAIRS_PER_ROUND
+ROUNDS_BEFORE_WEIGHTS = 2
 
 FLOPS = 2 * NODES * ROWS * CIN * COUT
 
@@ -38,7 +38,8 @@ def tile_linear_pa_t_e_kernel(tc, x, weights_words, weights_scales, path_weights
     with ExitStack() as ctx:
         ctx.enter_context(tc.manual_schedule())
         consts = ctx.enter_context(tc.tile_pool(name="consts", bufs=1))
-        x_pool = ctx.enter_context(tc.tile_pool(name="x", bufs=N_PAIRS))
+        x_first_pool = ctx.enter_context(tc.tile_pool(name="x_first", bufs=PAIRS_PER_ROUND))
+        x_pool = ctx.enter_context(tc.tile_pool(name="x", bufs=N_ROUNDS - 1))
         sorted_pool = ctx.enter_context(tc.tile_pool(name="sorted", bufs=3 * PAIRS_PER_ROUND))
         grouped_pool = ctx.enter_context(tc.tile_pool(name="grouped", bufs=2 * PAIRS_PER_ROUND))
         codes_pool = ctx.enter_context(tc.tile_pool(name="codes", bufs=3 * PAIRS_PER_ROUND))
@@ -78,14 +79,19 @@ def tile_linear_pa_t_e_kernel(tc, x, weights_words, weights_scales, path_weights
                 )
 
         x_pairs = []
-        for pair in range(N_PAIRS):
-            if pair == PAIRS_BEFORE_WEIGHTS:
+        for pair in range(PAIRS_PER_ROUND):
+            row = pair * PAIR
+            x_first = x_first_pool.tile([P, PAIR, CIN], BF16)
+            nc.sync.dma_start(out=x_first[:], in_=x[node_rows(0), row : row + PAIR, :])
+            x_pairs.append(x_first[:].bitcast(F32))
+        for r in range(1, N_ROUNDS):
+            if r == ROUNDS_BEFORE_WEIGHTS:
                 load_weights()
-            r = pair // PAIRS_PER_ROUND
-            row = first_row(r) + (pair % PAIRS_PER_ROUND) * PAIR
-            x_sb = x_pool.tile([P, PAIR, CIN], BF16)
-            nc.sync.dma_start(out=x_sb[:], in_=x[node_rows(r), row : row + PAIR, :])
-            x_pairs.append(x_sb)
+            row = first_row(r)
+            x_sb = x_pool.tile([P, ROUND, CIN], BF16)
+            nc.sync.dma_start(out=x_sb[:], in_=x[node_rows(r), row : row + ROUND, :])
+            for pair in range(PAIRS_PER_ROUND):
+                x_pairs.append(x_sb[:, pair * PAIR : (pair + 1) * PAIR, :].bitcast(F32))
 
         for l in range(DEGREES):
             rows_of_l = slice(l * l, (l + 1) * (l + 1))
@@ -100,7 +106,7 @@ def tile_linear_pa_t_e_kernel(tc, x, weights_words, weights_scales, path_weights
         def sort_pass_0(r):
             sorted_pairs = []
             for pair in pairs_of(r):
-                x_words = x_pairs[pair][:].bitcast(F32)
+                x_words = x_pairs[pair]
                 sorted_words = sorted_pool.tile([P, PAIR, HALVES, P], F32)
                 nc.vector.tensor_copy(
                     out=sorted_words[:],
@@ -112,7 +118,7 @@ def tile_linear_pa_t_e_kernel(tc, x, weights_words, weights_scales, path_weights
         def transpose_and_quantise(r, sorted_pairs):
             quantised = []
             for pair, sorted_words in zip(pairs_of(r), sorted_pairs):
-                x_words = x_pairs[pair][:].bitcast(F32)
+                x_words = x_pairs[pair]
                 grouped = grouped_pool.tile([P, PAIR, PASSES, P, PACK], BF16, align_bytes=64)
                 for s in range(PAIR):
                     turned = turned_pool.tile([P, PASSES, HALVES, P], F32)

@@ -22,13 +22,14 @@ assert PASSES == 2
 HALVES = 2
 QUADRANTS = 4
 
-PAIR = 2
 ROUND = 4
-PAIRS_PER_ROUND = ROUND // PAIR
+PAIR = 2
 ROUNDS_PER_NODE_TILE = ROWS // ROUND
 N_ROUNDS = (NODES // P) * ROUNDS_PER_NODE_TILE
-N_PAIRS = N_ROUNDS * PAIRS_PER_ROUND
 ROUNDS_BEFORE_WEIGHTS = 2
+FIRST_SORTED = 0
+END_SORTED = 16
+FINE_ROUNDS = 1
 
 FLOPS = 2 * NODES * ROWS * CIN * COUT
 
@@ -38,11 +39,11 @@ def tile_linear_pa_t_e_kernel(tc, x, weights_words, weights_scales, path_weights
     with ExitStack() as ctx:
         ctx.enter_context(tc.manual_schedule())
         consts = ctx.enter_context(tc.tile_pool(name="consts", bufs=1))
-        x_first_pool = ctx.enter_context(tc.tile_pool(name="x_first", bufs=PAIRS_PER_ROUND))
-        x_pool = ctx.enter_context(tc.tile_pool(name="x", bufs=N_ROUNDS - 1))
-        sorted_pool = ctx.enter_context(tc.tile_pool(name="sorted", bufs=3 * PAIRS_PER_ROUND))
-        grouped_pool = ctx.enter_context(tc.tile_pool(name="grouped", bufs=2 * PAIRS_PER_ROUND))
-        codes_pool = ctx.enter_context(tc.tile_pool(name="codes", bufs=3 * PAIRS_PER_ROUND))
+        x_fine_pool = ctx.enter_context(tc.tile_pool(name="x_fine", bufs=FINE_ROUNDS * ROUND // PAIR))
+        x_pool = ctx.enter_context(tc.tile_pool(name="x", bufs=N_ROUNDS - FINE_ROUNDS))
+        sorted_pool = ctx.enter_context(tc.tile_pool(name="sorted", bufs=3))
+        grouped_pool = ctx.enter_context(tc.tile_pool(name="grouped", bufs=2))
+        codes_pool = ctx.enter_context(tc.tile_pool(name="codes", bufs=3))
         result_pool = ctx.enter_context(tc.tile_pool(name="result", bufs=N_ROUNDS))
         turned_pool = ctx.enter_context(tc.psum_pool(name="turned", bufs=6))
         acc_pool = ctx.enter_context(tc.psum_pool(name="acc", bufs=2))
@@ -78,20 +79,21 @@ def tile_linear_pa_t_e_kernel(tc, x, weights_words, weights_scales, path_weights
                     .bitcast(I32),
                 )
 
-        x_pairs = []
-        for pair in range(PAIRS_PER_ROUND):
-            row = pair * PAIR
-            x_first = x_first_pool.tile([P, PAIR, CIN], BF16)
-            nc.sync.dma_start(out=x_first[:], in_=x[node_rows(0), row : row + PAIR, :])
-            x_pairs.append(x_first[:].bitcast(F32))
-        for r in range(1, N_ROUNDS):
+        x_words = []
+        for r in range(N_ROUNDS):
             if r == ROUNDS_BEFORE_WEIGHTS:
                 load_weights()
-            row = first_row(r)
-            x_sb = x_pool.tile([P, ROUND, CIN], BF16)
-            nc.sync.dma_start(out=x_sb[:], in_=x[node_rows(r), row : row + ROUND, :])
-            for pair in range(PAIRS_PER_ROUND):
-                x_pairs.append(x_sb[:, pair * PAIR : (pair + 1) * PAIR, :].bitcast(F32))
+            n = PAIR if r < FINE_ROUNDS else ROUND
+            words = []
+            for first in range(0, ROUND, n):
+                row = first_row(r) + first
+                if r < FINE_ROUNDS:
+                    x_sb = x_fine_pool.tile([P, n, CIN], BF16, name="x_fine")
+                else:
+                    x_sb = x_pool.tile([P, n, CIN], BF16)
+                nc.sync.dma_start(out=x_sb[:], in_=x[node_rows(r), row : row + n, :])
+                words.append(x_sb[:].bitcast(F32))
+            x_words.append(words)
 
         for l in range(DEGREES):
             rows_of_l = slice(l * l, (l + 1) * (l + 1))
@@ -100,84 +102,122 @@ def tile_linear_pa_t_e_kernel(tc, x, weights_words, weights_scales, path_weights
                 in_=factor_of_degree[:, l : l + 1].to_broadcast([P, 2 * l + 1]),
             )
 
-        def pairs_of(r):
-            return range(r * PAIRS_PER_ROUND, (r + 1) * PAIRS_PER_ROUND)
+        sorted_of = {}
+        grouped_of = {}
+        quantised_of = {}
+        acc_of = {}
+        result_of = {}
 
         def sort_pass_0(r):
-            sorted_pairs = []
-            for pair in pairs_of(r):
-                x_words = x_pairs[pair]
-                sorted_words = sorted_pool.tile([P, PAIR, HALVES, P], F32)
+            if not FIRST_SORTED <= r < END_SORTED:
+                return
+            sorted_words = sorted_pool.tile([P, ROUND, HALVES, P], F32)
+            n = ROUND // len(x_words[r])
+            for first in range(0, ROUND, PAIR):
+                piece = x_words[r][first // n]
                 nc.vector.tensor_copy(
-                    out=sorted_words[:],
-                    in_=x_words[:, :, 0 : K_PASS // 2].rearrange("p s (j u) -> p s u j", u=HALVES),
+                    out=sorted_words[:, first : first + PAIR],
+                    in_=piece[:, first % n : first % n + PAIR, 0 : K_PASS // 2].rearrange("p s (j u) -> p s u j", u=HALVES),
                 )
-                sorted_pairs.append(sorted_words)
-            return sorted_pairs
+            sorted_of[r] = sorted_words
 
-        def transpose_and_quantise(r, sorted_pairs):
-            quantised = []
-            for pair, sorted_words in zip(pairs_of(r), sorted_pairs):
-                x_words = x_pairs[pair]
-                grouped = grouped_pool.tile([P, PAIR, PASSES, P, PACK], BF16, align_bytes=64)
-                for s in range(PAIR):
-                    turned = turned_pool.tile([P, PASSES, HALVES, P], F32)
-                    for u in range(HALVES):
-                        nc.tensor.transpose(turned[:, 0, u, :], sorted_words[:, s, u, :], identity[:])
-                    for u in range(HALVES):
-                        nc.tensor.transpose(
-                            turned[:, 1, u, :],
-                            x_words[:, s, K_PASS // 2 + u : K_PASS : HALVES],
-                            identity[:],
-                        )
-                    nc.scalar.copy(
-                        out=grouped[:, s].bitcast(F32),
-                        in_=turned[:].rearrange("p g u n -> p g n u"),
-                    )
-                codes = codes_pool.tile([P, PAIR, PASSES, P], U32, align_bytes=64)
-                scales = codes_pool.tile([P, PAIR, PASSES, P], U8, align_bytes=64)
-                nc.vector.quantize_mx(
-                    out=codes[:].rearrange("p s g n -> p (s g n)").bitcast(FP8X4),
-                    scales=scales[:].rearrange("p s g n -> p (s g n)"),
-                    in_=grouped[:].rearrange("p s g n t -> p (s g n t)"),
+        def transpose(r):
+            grouped = grouped_pool.tile([P, ROUND, PASSES, P, PACK], BF16, align_bytes=64)
+            grouped_of[r] = grouped
+            n = ROUND // len(x_words[r])
+            for i in range(ROUND):
+                words = x_words[r][i // n][:, i % n, :]
+                turned = turned_pool.tile([P, PASSES, HALVES, P], F32)
+                for u in range(HALVES):
+                    if r in sorted_of:
+                        nc.tensor.transpose(turned[:, 0, u, :], sorted_of[r][:, i, u, :], identity[:])
+                    else:
+                        nc.tensor.transpose(turned[:, 0, u, :], words[:, u : K_PASS // 2 : HALVES], identity[:])
+                for u in range(HALVES):
+                    nc.tensor.transpose(turned[:, 1, u, :], words[:, K_PASS // 2 + u : K_PASS : HALVES], identity[:])
+                nc.scalar.copy(
+                    out=grouped[:, i].bitcast(F32),
+                    in_=turned[:].rearrange("p g u n -> p g n u"),
                 )
-                quantised.append((codes, scales))
-            return quantised
 
-        def multiply_and_store(r, quantised):
-            acc = acc_pool.tile([P, ROUND, COUT], F32)
-            for slab in range(ROUND):
-                codes, scales = quantised[slab // PAIR]
-                s = slab % PAIR
-                l = DEGREE_OF_ROW[first_row(r) + slab]
+        def quantise(r, first, count):
+            if first == 0:
+                codes = codes_pool.tile([P, ROUND, PASSES, P], U32, align_bytes=64)
+                scales = codes_pool.tile([P, ROUND, PASSES, P], U8, align_bytes=64)
+                quantised_of[r] = (codes, scales)
+            codes, scales = quantised_of[r]
+            part = slice(first, first + count)
+            nc.vector.quantize_mx(
+                out=codes[:, part].rearrange("p s g n -> p (s g n)").bitcast(FP8X4),
+                scales=scales[:, part].rearrange("p s g n -> p (s g n)"),
+                in_=grouped_of[r][:, part].rearrange("p s g n t -> p (s g n t)"),
+            )
+
+        def multiply(r, first, count, own_bank=False):
+            if first == 0:
+                acc = acc_pool.tile([P, ROUND, COUT], F32)
+                acc_of[r] = acc
+            if own_bank:
+                turned = turned_pool.tile([P, ROUND, COUT], F32)
+                acc_of[r] = turned
+            codes, scales = quantised_of[r]
+            for i in range(first, first + count):
+                l = DEGREE_OF_ROW[first_row(r) + i]
                 for g in range(PASSES):
                     nc.tensor.matmul_mx(
-                        out=acc[:, slab, :],
-                        lhsT=codes[:, s, g, :].bitcast(FP8X4),
-                        lhsT_scale=scales[:, s, g, :],
+                        out=acc_of[r][:, i, :],
+                        lhsT=codes[:, i, g, :].bitcast(FP8X4),
+                        lhsT_scale=scales[:, i, g, :],
                         rhs=w_codes[:, l * PASSES + g, :].bitcast(FP8X4),
                         rhs_scale=w_scales[:, l * PASSES + g, :],
                         start=(g == 0),
                         stop=(g == PASSES - 1),
                     )
-            rows = slice(first_row(r), first_row(r) + ROUND)
-            result = result_pool.tile([P, ROUND, COUT], F32)
-            nc.vector.tensor_tensor(
-                out=result[:],
-                in0=acc[:],
-                in1=factor_of_row[:, rows].unsqueeze(2).to_broadcast([P, ROUND, COUT]),
-                op=mybir.AluOpType.mult,
-            )
-            nc.sync.dma_start(out=out[node_rows(r), rows, :], in_=result[:])
 
-        sorted_ahead = sort_pass_0(0)
-        waiting = None
-        for r in range(N_ROUNDS):
-            sorted_now = sorted_ahead
-            if r + 1 < N_ROUNDS:
-                sorted_ahead = sort_pass_0(r + 1)
-            quantised = transpose_and_quantise(r, sorted_now)
-            if waiting is not None:
-                multiply_and_store(r - 1, waiting)
-            waiting = quantised
-        multiply_and_store(N_ROUNDS - 1, waiting)
+        def scale_and_store(r, first, count, on_scalar):
+            if first == 0:
+                result = result_pool.tile([P, ROUND, COUT], F32)
+                result_of[r] = result
+            result = result_of[r]
+            row = first_row(r) + first
+            if on_scalar:
+                for l in range(DEGREES):
+                    of_l = [i for i in range(first, first + count) if DEGREE_OF_ROW[first_row(r) + i] == l]
+                    if of_l:
+                        i, j = of_l[0], of_l[-1] + 1
+                        nc.scalar.activation(
+                            out=result[:, i:j, :],
+                            in_=acc_of[r][:, i:j, :],
+                            func=mybir.ActivationFunctionType.Copy,
+                            scale=factor_of_row[:, first_row(r) + i : first_row(r) + i + 1],
+                        )
+            else:
+                nc.vector.tensor_tensor(
+                    out=result[:, first : first + count, :],
+                    in0=acc_of[r][:, first : first + count, :],
+                    in1=factor_of_row[:, row : row + count].unsqueeze(2).to_broadcast([P, count, COUT]),
+                    op=mybir.AluOpType.mult,
+                )
+            nc.sync.dma_start(out=out[node_rows(r), row : row + count, :], in_=result[:, first : first + count, :])
+
+        LAST = N_ROUNDS - 1
+        sort_pass_0(0)
+        for r in range(LAST):
+            sort_pass_0(r + 1)
+            transpose(r)
+            quantise(r, 0, PAIR)
+            quantise(r, PAIR, PAIR)
+            if r > 0:
+                multiply(r - 1, 0, ROUND)
+                scale_and_store(r - 1, 0, ROUND, False)
+        transpose(LAST)
+        quantise(LAST, 0, PAIR)
+        multiply(LAST - 1, 0, ROUND)
+        scale_and_store(LAST - 1, 0, ROUND, True)
+        quantise(LAST, 2, 1)
+        quantise(LAST, 3, 1)
+        multiply(LAST, 0, PAIR)
+        multiply(LAST, 2, 1)
+        scale_and_store(LAST, 0, 3, False)
+        multiply(LAST, 3, 1, own_bank=True)
+        scale_and_store(LAST, 3, 1, False)

@@ -41,7 +41,7 @@ def tile_linear_pa_t_e_kernel(tc, x, weights_words, weights_scales, path_weights
         consts = ctx.enter_context(tc.tile_pool(name="consts", bufs=1))
         x_fine_pool = ctx.enter_context(tc.tile_pool(name="x_fine", bufs=FINE_ROUNDS * ROUND // PAIR))
         x_pool = ctx.enter_context(tc.tile_pool(name="x", bufs=N_ROUNDS - FINE_ROUNDS))
-        sorted_pool = ctx.enter_context(tc.tile_pool(name="sorted", bufs=3))
+        sorted_pool = ctx.enter_context(tc.tile_pool(name="sorted", bufs=4))
         grouped_pool = ctx.enter_context(tc.tile_pool(name="grouped", bufs=2))
         codes_pool = ctx.enter_context(tc.tile_pool(name="codes", bufs=3))
         result_pool = ctx.enter_context(tc.tile_pool(name="result", bufs=N_ROUNDS))
@@ -202,11 +202,13 @@ def tile_linear_pa_t_e_kernel(tc, x, weights_words, weights_scales, path_weights
 
         LAST = N_ROUNDS - 1
         sort_pass_0(0)
+        sort_pass_0(1)
         for r in range(LAST):
-            sort_pass_0(r + 1)
             transpose(r)
             quantise(r, 0, PAIR)
             quantise(r, PAIR, PAIR)
+            if r + 2 <= LAST:
+                sort_pass_0(r + 2)
             if r > 0:
                 multiply(r - 1, 0, ROUND)
                 scale_and_store(r - 1, 0, ROUND, False)

@@ -44,7 +44,7 @@ def tile_linear_pa_t_e_kernel(tc, x, weights_words, weights_scales, path_weights
         sorted_pool = ctx.enter_context(tc.tile_pool(name="sorted", bufs=4))
         grouped_pool = ctx.enter_context(tc.tile_pool(name="grouped", bufs=2))
         codes_pool = ctx.enter_context(tc.tile_pool(name="codes", bufs=3))
-        result_pool = ctx.enter_context(tc.tile_pool(name="result", bufs=N_ROUNDS))
+        result_pool = ctx.enter_context(tc.tile_pool(name="result", bufs=NODES // P))
         turned_pool = ctx.enter_context(tc.psum_pool(name="turned", bufs=6))
         acc_pool = ctx.enter_context(tc.psum_pool(name="acc", bufs=2))
 
@@ -175,10 +175,11 @@ def tile_linear_pa_t_e_kernel(tc, x, weights_words, weights_scales, path_weights
                     )
 
         def scale_and_store(r, first, count, on_scalar):
-            if first == 0:
-                result = result_pool.tile([P, ROUND, COUT], F32)
-                result_of[r] = result
-            result = result_of[r]
+            node_tile = r // ROUNDS_PER_NODE_TILE
+            if first == 0 and first_row(r) == 0:
+                result = result_pool.tile([P, ROWS, COUT], F32)
+                result_of[node_tile] = result
+            result = result_of[node_tile][:, first_row(r) : first_row(r) + ROUND, :]
             row = first_row(r) + first
             if on_scalar:
                 for l in range(DEGREES):
@@ -198,7 +199,11 @@ def tile_linear_pa_t_e_kernel(tc, x, weights_words, weights_scales, path_weights
                     in1=factor_of_row[:, row : row + count].unsqueeze(2).to_broadcast([P, count, COUT]),
                     op=mybir.AluOpType.mult,
                 )
-            nc.sync.dma_start(out=out[node_rows(r), row : row + count, :], in_=result[:, first : first + count, :])
+            if node_tile < NODES // P - 1:
+                if row + count == ROWS:
+                    nc.sync.dma_start(out=out[node_rows(r), :, :], in_=result_of[node_tile][:])
+            else:
+                nc.sync.dma_start(out=out[node_rows(r), row : row + count, :], in_=result[:, first : first + count, :])
 
         LAST = N_ROUNDS - 1
         sort_pass_0(0)

@@ -26,6 +26,7 @@ ROUND = 4
 PAIR = 2
 ROUNDS_PER_NODE_TILE = ROWS // ROUND
 N_ROUNDS = (NODES // P) * ROUNDS_PER_NODE_TILE
+ROUNDS_BEFORE_SCALES = 1
 ROUNDS_BEFORE_WEIGHTS = 2
 FIRST_SORTED = 0
 END_SORTED = 16
@@ -58,19 +59,24 @@ def tile_linear_pa_t_e_kernel(tc, x, weights_words, weights_scales, path_weights
         identity = consts.tile([P, P], F32)
         make_identity(nc, identity[:])
 
-        factor_of_degree = consts.tile([P, DEGREES], BF16)
-        nc.scalar.dma_start(out=factor_of_degree[:], in_=path_weights.partition_broadcast(P))
+        ones = consts.tile([P, P], BF16)
+        nc.gpsimd.memset(ones[:], 1.0)
+        factor_row = consts.tile([P, DEGREES], BF16)
+        nc.vector.memset(factor_row[:], 0.0)
+        nc.scalar.dma_start(out=factor_row[0:1, :], in_=path_weights.unsqueeze(0))
         factor_of_row = consts.tile([P, ROWS], F32)
 
         w_codes = consts.tile([P, DEGREES * PASSES, COUT], U32, align_bytes=64)
         w_scales = consts.tile([P, DEGREES * PASSES, COUT], U8, align_bytes=64)
         nc.vector.memset(w_scales[:].bitcast(I32), 0)
 
-        def load_weights():
+        def load_weight_codes():
             nc.sync.dma_start(
                 out=w_codes[:].bitcast(I32),
                 in_=weights_words.rearrange("g p n t -> p g (n t)").bitcast(I32),
             )
+
+        def load_weight_scales():
             for quadrant in range(QUADRANTS):
                 nc.sync.dma_start(
                     out=w_scales[32 * quadrant : 32 * quadrant + 4, :, :].bitcast(I32),
@@ -81,8 +87,10 @@ def tile_linear_pa_t_e_kernel(tc, x, weights_words, weights_scales, path_weights
 
         x_words = []
         for r in range(N_ROUNDS):
+            if r == ROUNDS_BEFORE_SCALES:
+                load_weight_scales()
             if r == ROUNDS_BEFORE_WEIGHTS:
-                load_weights()
+                load_weight_codes()
             n = PAIR if r < FINE_ROUNDS else ROUND
             words = []
             for first in range(0, ROUND, n):
@@ -95,12 +103,15 @@ def tile_linear_pa_t_e_kernel(tc, x, weights_words, weights_scales, path_weights
                 words.append(x_sb[:].bitcast(F32))
             x_words.append(words)
 
-        for l in range(DEGREES):
-            rows_of_l = slice(l * l, (l + 1) * (l + 1))
-            nc.vector.tensor_copy(
-                out=factor_of_row[:, rows_of_l],
-                in_=factor_of_degree[:, l : l + 1].to_broadcast([P, 2 * l + 1]),
-            )
+        def spread_factors():
+            factor_of_degree = acc_pool.tile([P, DEGREES], F32, name="acc")
+            nc.tensor.matmul(out=factor_of_degree[:], lhsT=ones[:], rhs=factor_row[:], start=True, stop=True)
+            for l in range(DEGREES):
+                rows_of_l = slice(l * l, (l + 1) * (l + 1))
+                nc.vector.tensor_copy(
+                    out=factor_of_row[:, rows_of_l],
+                    in_=factor_of_degree[:, l : l + 1].to_broadcast([P, 2 * l + 1]),
+                )
 
         sorted_of = {}
         grouped_of = {}
@@ -212,6 +223,8 @@ def tile_linear_pa_t_e_kernel(tc, x, weights_words, weights_scales, path_weights
             transpose(r)
             quantise(r, 0, PAIR)
             quantise(r, PAIR, PAIR)
+            if r == 0:
+                spread_factors()
             if r + 2 <= LAST:
                 sort_pass_0(r + 2)
             if r > 0:

from contextlib import ExitStack

import concourse.mybir as mybir
from concourse.masks import make_identity

BF16 = mybir.dt.bfloat16
F32 = mybir.dt.float32
I32 = mybir.dt.int32
U32 = mybir.dt.uint32
U8 = mybir.dt.uint8
FP8X4 = mybir.dt.float8_e4m3fn_x4

NODES, ROWS, CIN, COUT, DEGREES = 512, 16, 1024, 128, 4
DEGREE_OF_ROW = [l for l in range(DEGREES) for i in range(2 * l + 1)]
assert len(DEGREE_OF_ROW) == ROWS

P = 128
PACK = 4
K_PASS = P * PACK
PASSES = CIN // K_PASS
assert PASSES == 2
HALVES = 2
QUADRANTS = 4

ROUND = 4
PAIR = 2
ROUNDS_PER_NODE_TILE = ROWS // ROUND
N_ROUNDS = (NODES // P) * ROUNDS_PER_NODE_TILE
ROUNDS_BEFORE_SCALES = 1
ROUNDS_BEFORE_WEIGHTS = 2
FIRST_SORTED = 0
END_SORTED = 16
FINE_ROUNDS = 1

FLOPS = 2 * NODES * ROWS * CIN * COUT


def tile_linear_pa_t_e_kernel(tc, x, weights_words, weights_scales, path_weights, out):
    nc = tc.nc
    with ExitStack() as ctx:
        ctx.enter_context(tc.manual_schedule())
        consts = ctx.enter_context(tc.tile_pool(name="consts", bufs=1))
        x_fine_pool = ctx.enter_context(tc.tile_pool(name="x_fine", bufs=FINE_ROUNDS * ROUND // PAIR))
        x_pool = ctx.enter_context(tc.tile_pool(name="x", bufs=N_ROUNDS - FINE_ROUNDS))
        sorted_pool = ctx.enter_context(tc.tile_pool(name="sorted", bufs=4))
        grouped_pool = ctx.enter_context(tc.tile_pool(name="grouped", bufs=2))
        codes_pool = ctx.enter_context(tc.tile_pool(name="codes", bufs=3))
        result_pool = ctx.enter_context(tc.tile_pool(name="result", bufs=NODES // P))
        turned_pool = ctx.enter_context(tc.psum_pool(name="turned", bufs=6))
        acc_pool = ctx.enter_context(tc.psum_pool(name="acc", bufs=2))

        def node_rows(r):
            first = (r // ROUNDS_PER_NODE_TILE) * P
            return slice(first, first + P)

        def first_row(r):
            return (r % ROUNDS_PER_NODE_TILE) * ROUND

        identity = consts.tile([P, P], F32)
        make_identity(nc, identity[:])

        ones = consts.tile([P, P], BF16)
        nc.gpsimd.memset(ones[:], 1.0)
        factor_row = consts.tile([P, DEGREES], BF16)
        nc.vector.memset(factor_row[:], 0.0)
        nc.scalar.dma_start(out=factor_row[0:1, :], in_=path_weights.unsqueeze(0))
        factor_of_row = consts.tile([P, ROWS], F32)

        w_codes = consts.tile([P, DEGREES * PASSES, COUT], U32, align_bytes=64)
        w_scales = consts.tile([P, DEGREES * PASSES, COUT], U8, align_bytes=64)
        nc.vector.memset(w_scales[:].bitcast(I32), 0)

        def load_weight_codes():
            nc.sync.dma_start(
                out=w_codes[:].bitcast(I32),
                in_=weights_words.rearrange("g p n t -> p g (n t)").bitcast(I32),
            )

        def load_weight_scales():
            for quadrant in range(QUADRANTS):
                nc.sync.dma_start(
                    out=w_scales[32 * quadrant : 32 * quadrant + 4, :, :].bitcast(I32),
                    in_=weights_scales[:, 4 * quadrant : 4 * quadrant + 4, :]
                    .rearrange("g r n -> r g n")
                    .bitcast(I32),
                )

        x_words = []
        for r in range(N_ROUNDS):
            if r == ROUNDS_BEFORE_SCALES:
                load_weight_scales()
            if r == ROUNDS_BEFORE_WEIGHTS:
                load_weight_codes()
            n = PAIR if r < FINE_ROUNDS else ROUND
            words = []
            for first in range(0, ROUND, n):
                row = first_row(r) + first
                if r < FINE_ROUNDS:
                    x_sb = x_fine_pool.tile([P, n, CIN], BF16, name="x_fine")
                else:
                    x_sb = x_pool.tile([P, n, CIN], BF16)
                nc.sync.dma_start(out=x_sb[:], in_=x[node_rows(r), row : row + n, :])
                words.append(x_sb[:].bitcast(F32))
            x_words.append(words)

        def spread_factors():
            factor_of_degree = acc_pool.tile([P, DEGREES], F32, name="acc")
            nc.tensor.matmul(out=factor_of_degree[:], lhsT=ones[:], rhs=factor_row[:], start=True, stop=True)
            for l in range(DEGREES):
                rows_of_l = slice(l * l, (l + 1) * (l + 1))
                nc.vector.tensor_copy(
                    out=factor_of_row[:, rows_of_l],
                    in_=factor_of_degree[:, l : l + 1].to_broadcast([P, 2 * l + 1]),
                )

        sorted_of = {}
        grouped_of = {}
        quantised_of = {}
        acc_of = {}
        result_of = {}

        def sort_pass_0(r):
            if not FIRST_SORTED <= r < END_SORTED:
                return
            sorted_words = sorted_pool.tile([P, ROUND, HALVES, P], F32)
            n = ROUND // len(x_words[r])
            for first in range(0, ROUND, PAIR):
                piece = x_words[r][first // n]
                nc.vector.tensor_copy(
                    out=sorted_words[:, first : first + PAIR],
                    in_=piece[:, first % n : first % n + PAIR, 0 : K_PASS // 2].rearrange("p s (j u) -> p s u j", u=HALVES),
                )
            sorted_of[r] = sorted_words

        def transpose(r):
            grouped = grouped_pool.tile([P, ROUND, PASSES, P, PACK], BF16, align_bytes=64)
            grouped_of[r] = grouped
            n = ROUND // len(x_words[r])
            for i in range(ROUND):
                words = x_words[r][i // n][:, i % n, :]
                turned = turned_pool.tile([P, PASSES, HALVES, P], F32)
                for u in range(HALVES):
                    if r in sorted_of:
                        nc.tensor.transpose(turned[:, 0, u, :], sorted_of[r][:, i, u, :], identity[:])
                    else:
                        nc.tensor.transpose(turned[:, 0, u, :], words[:, u : K_PASS // 2 : HALVES], identity[:])
                for u in range(HALVES):
                    nc.tensor.transpose(turned[:, 1, u, :], words[:, K_PASS // 2 + u : K_PASS : HALVES], identity[:])
                nc.scalar.copy(
                    out=grouped[:, i].bitcast(F32),
                    in_=turned[:].rearrange("p g u n -> p g n u"),
                )

        def quantise(r, first, count):
            if first == 0:
                codes = codes_pool.tile([P, ROUND, PASSES, P], U32, align_bytes=64)
                scales = codes_pool.tile([P, ROUND, PASSES, P], U8, align_bytes=64)
                quantised_of[r] = (codes, scales)
            codes, scales = quantised_of[r]
            part = slice(first, first + count)
            nc.vector.quantize_mx(
                out=codes[:, part].rearrange("p s g n -> p (s g n)").bitcast(FP8X4),
                scales=scales[:, part].rearrange("p s g n -> p (s g n)"),
                in_=grouped_of[r][:, part].rearrange("p s g n t -> p (s g n t)"),
            )

        def multiply(r, first, count, own_bank=False):
            if first == 0:
                acc = acc_pool.tile([P, ROUND, COUT], F32)
                acc_of[r] = acc
            if own_bank:
                turned = turned_pool.tile([P, ROUND, COUT], F32)
                acc_of[r] = turned
            codes, scales = quantised_of[r]
            for i in range(first, first + count):
                l = DEGREE_OF_ROW[first_row(r) + i]
                for g in range(PASSES):
                    nc.tensor.matmul_mx(
                        out=acc_of[r][:, i, :],
                        lhsT=codes[:, i, g, :].bitcast(FP8X4),
                        lhsT_scale=scales[:, i, g, :],
                        rhs=w_codes[:, l * PASSES + g, :].bitcast(FP8X4),
                        rhs_scale=w_scales[:, l * PASSES + g, :],
                        start=(g == 0),
                        stop=(g == PASSES - 1),
                    )

        def scale_and_store(r, first, count, on_scalar):
            node_tile = r // ROUNDS_PER_NODE_TILE
            if first == 0 and first_row(r) == 0:
                result = result_pool.tile([P, ROWS, COUT], F32)
                result_of[node_tile] = result
            result = result_of[node_tile][:, first_row(r) : first_row(r) + ROUND, :]
            row = first_row(r) + first
            if on_scalar:
                for l in range(DEGREES):
                    of_l = [i for i in range(first, first + count) if DEGREE_OF_ROW[first_row(r) + i] == l]
                    if of_l:
                        i, j = of_l[0], of_l[-1] + 1
                        nc.scalar.activation(
                            out=result[:, i:j, :],
                            in_=acc_of[r][:, i:j, :],
                            func=mybir.ActivationFunctionType.Copy,
                            scale=factor_of_row[:, first_row(r) + i : first_row(r) + i + 1],
                        )
            else:
                nc.vector.tensor_tensor(
                    out=result[:, first : first + count, :],
                    in0=acc_of[r][:, first : first + count, :],
                    in1=factor_of_row[:, row : row + count].unsqueeze(2).to_broadcast([P, count, COUT]),
                    op=mybir.AluOpType.mult,
                )
            if node_tile < NODES // P - 1:
                if row + count == ROWS:
                    nc.sync.dma_start(out=out[node_rows(r), :, :], in_=result_of[node_tile][:])
            else:
                nc.sync.dma_start(out=out[node_rows(r), row : row + count, :], in_=result[:, first : first + count, :])

        LAST = N_ROUNDS - 1
        sort_pass_0(0)
        sort_pass_0(1)
        for r in range(LAST):
            transpose(r)
            quantise(r, 0, PAIR)
            quantise(r, PAIR, PAIR)
            if r == 0:
                spread_factors()
            if r + 2 <= LAST:
                sort_pass_0(r + 2)
            if r > 0:
                multiply(r - 1, 0, ROUND)
                scale_and_store(r - 1, 0, ROUND, False)
        transpose(LAST)
        quantise(LAST, 0, PAIR)
        multiply(LAST - 1, 0, ROUND)
        scale_and_store(LAST - 1, 0, ROUND, True)
        quantise(LAST, 2, 1)
        quantise(LAST, 3, 1)
        multiply(LAST, 0, PAIR)
        multiply(LAST, 2, 1)
        scale_and_store(LAST, 0, 3, False)
        multiply(LAST, 3, 1, own_bank=True)
        scale_and_store(LAST, 3, 1, False)
